import numpy as np
import ml_dtypes


def mxq(x, axis, fmt="e4m3"):
    dtype, down = {"e4m3": (ml_dtypes.float8_e4m3fn, 7), "e5m2": (ml_dtypes.float8_e5m2, 14)}[fmt]
    v = np.moveaxis(np.asarray(x, np.float32).astype(ml_dtypes.bfloat16).astype(np.float64), axis, -1)
    blocks = v.reshape(v.shape[:-1] + (-1, 32))
    amax = np.abs(blocks).max(-1, keepdims=True)
    byte = np.maximum(np.where(amax > 0, np.frexp(amax)[1] - 1 + 127, 0) - down, 1)
    scale = np.exp2(byte - 127.0)
    codes = (blocks / scale).astype(np.float32).astype(dtype).astype(np.float64)
    return np.moveaxis((codes * scale).reshape(v.shape), -1, axis)


WIDE = False


def mx_kscale(k):
    if not WIDE:
        return np.ones(k)
    levels = np.array([18, -18])
    if k % 512:
        return np.exp2(np.random.permutation(np.resize(levels, k // 32))).repeat(32)
    a = np.empty((k // 512, 16))
    for p in range(k // 512):
        a[p, :8] = np.random.permutation(np.resize(levels, 8))
        for g in range(8):
            far = levels[np.abs(levels - a[p, g]) >= 10]
            a[p, g + 8] = far[np.random.randint(len(far))]
    return np.exp2(a.ravel()).repeat(32)


BF16 = ml_dtypes.bfloat16


def bf(x):
    return np.asarray(x, np.float32).astype(BF16)


def f64(x):
    return np.asarray(x).astype(np.float64)


B, CK, CV, NO, T, H, W = 1, 128, 512, 3, 4, 32, 16
N = T * H * W
P = H * W
C = NO * CV


def softmax_affinity(mk, mksq, qk, qe, qs, ms):
    a_sq = f64(mksq).transpose(0, 2, 1) @ f64(qe)
    two_ab = 2.0 * (f64(mk).transpose(0, 2, 1) @ f64(qs))
    b_sq = np.sum(f64(qs) * f64(qk), axis=1, keepdims=True)
    similarity = (-a_sq + two_ab - b_sq) * f64(ms)[:, :, None] * (1.0 / np.sqrt(CK))
    e = np.exp(similarity - similarity.max(axis=1, keepdims=True))
    return e / e.sum(axis=1, keepdims=True)


def setup_inputs():
    u = mx_kscale(C)
    v = mx_kscale(P)
    s = mx_kscale(N)
    mk = bf(np.random.standard_normal((B, CK, N)))
    qk = bf(np.random.standard_normal((B, CK, P)))
    qe0 = bf(np.random.uniform(0.0, 1.0, (B, CK, P)))
    ms0 = bf(0.75 + 0.5 * np.random.uniform(0.0, 1.0, (B, N)))
    mv0 = bf(np.random.standard_normal((B, C, N)))
    mksq0 = bf(f64(mk) * f64(mk))
    qs = bf(f64(qk) * f64(qe0))
    g = bf(16.0 * np.random.standard_normal((B, C, P)) * np.exp2(np.random.randint(-6, 1, (B, 1, P))) * u[None, :, None] * v[None, None, :])
    affinity = softmax_affinity(mk, mksq0, qk, qe0, qs, ms0)
    return {"memory_key": mk,
            "memory_key_sq": bf(f64(mksq0) * s[None, None, :]),
            "query_key": qk,
            "query_selection": bf(f64(qe0) / v[None, None, :]),
            "query_key_sel": qs,
            "memory_shrinkage": bf(f64(ms0) / s[None, :]),
            "memory_value": bf(f64(mv0) / u[None, :, None]),
            "affinity": np.asarray(affinity, np.float32),
            "grad_out": g}


def reference(memory_key, memory_key_sq, query_key, query_selection, query_key_sel, memory_shrinkage, memory_value, affinity, grad_out):
    a = f64(affinity)
    da = mxq(f64(memory_value), 1, "e4m3").transpose(0, 2, 1) @ mxq(f64(grad_out), 1, "e5m2")
    dsim = a * (da - np.sum(a * da, axis=1, keepdims=True))
    dz = -dsim * f64(memory_shrinkage)[:, :, None] * (1.0 / np.sqrt(CK))
    dmksq = mxq(f64(query_selection), 2, "e4m3") @ mxq(dz, 2, "e5m2").transpose(0, 2, 1)
    dqe = mxq(f64(memory_key_sq), 2, "e4m3") @ mxq(dz, 1, "e5m2")
    return dmksq, dqe

@@ -1,0 +1,399 @@
+from contextlib import ExitStack
+
+import concourse.mybir as mybir
+from concourse.masks import make_identity
+
+F32 = mybir.dt.float32
+BF16 = mybir.dt.bfloat16
+U32 = mybir.dt.uint32
+U8 = mybir.dt.uint8
+E4 = mybir.dt.float8_e4m3fn_x4
+E5 = mybir.dt.float8_e5m2_x4
+ALU = mybir.AluOpType
+AX = mybir.AxisListType
+
+C, N, P, CK = 1536, 2048, 512, 128
+FLOPS = 2 * N * P * C + 2 * 2 * CK * P * N
+BYTES = 2 * (CK * N + CK * P + N + C * N + C * P) + 4 * (N * P + CK * N + CK * P)
+C2V = 128
+RAWB = 15
+LOADS = "m00 ms m01 m02 m12 m11 m10 a0 m20 m21 m22 a1 m30 m31 m32 a2 mk a3 qe"
+SEQ1 = "t0 t1 B A C P Q0 d0 Q1 d1 D t2 d2 d3 t3 n0 v0 n1 v1 Q2 v2 v3 n2"
+APG = {1: 0, 2: 1, 3:2}
+SEQ2 = "x0 x1 M w0 x2 x3 W0 A Z N p1 J p0 p3 p2 o w1 I O a W1"
+AP2 = {0: 3}
+WV = {(3, 1)}
+IV = {3: 512-64}
+APE = "V"
+
+
+def tile_vidsam_pa_v_kernel(tc, mk, mksq, qk, qe, qks, ms, mv, aff, gout, out_0, out_1):
+    nc = tc.nc
+    V, S, T = nc.vector, nc.scalar, nc.tensor
+    mksq2 = mksq.rearrange("b c n -> (b c) n")
+    qe2 = qe.rearrange("b c n -> (b c) n")
+    mv2 = mv.rearrange("b c n -> (b c) n")
+    g2 = gout.rearrange("b c n -> (b c) n")
+    a2 = aff.rearrange("b c n -> (b c) n")
+    o0 = out_0.rearrange("b c n -> (b c) n")
+    o1 = out_1.rearrange("b c n -> (b c) n")
+    with ExitStack() as ctx:
+        keep = ctx.enter_context(tc.tile_pool(name="keep", bufs=1))
+        rot = ctx.enter_context(tc.tile_pool(name="rot", bufs=2))
+        psum = ctx.enter_context(tc.psum_pool(name="psum", bufs=4))
+        ctx.enter_context(tc.manual_schedule())
+
+        def bank(tag):
+            return psum.tile([128, 512], F32, name=tag, tag=tag, bufs=4)
+
+        def raw_tile():
+            return rot.tile([128, 4, 512], BF16, name="raw", tag="raw", bufs=RAWB, align_bytes=64)
+
+        def grp_tile():
+            return rot.tile([128, 2048], BF16, name="grp", tag="grp", bufs=5, align_bytes=64)
+
+        def codes(name):
+            c = keep.tile([128, 512], U32, name=name, tag=name, align_bytes=64)
+            s = keep.tile([128, 512], U8, name=name + "s", tag=name + "s", align_bytes=64)
+            return c, s
+
+        graw, mraw, araw = [], {}, {}
+        for c in range(3):
+            r = raw_tile()
+            nc.sync.dma_start(out=r[:], in_=g2[512 * c : 512 * c + 512, :].rearrange("(p j) w -> p j w", j=4))
+            graw.append(r)
+
+        def load_a(g):
+            t = rot.tile([128, 4, 512], F32, name="aff", tag="aff", bufs=6, align_bytes=64)
+            nc.sync.dma_start(out=t[:], in_=a2[512 * g : 512 * g + 512, :].rearrange("(p k) w -> p k w", k=4))
+            araw[g] = t
+
+        msb = keep.tile([128, 4, 4], BF16, name="msb", tag="msb")
+        mksb = keep.tile([128, 2048], BF16, name="mksb", tag="mksb", align_bytes=64)
+        qesb = keep.tile([128, 512], BF16, name="qesb", tag="qesb", align_bytes=64)
+
+        def load_mv(g, c):
+            r = raw_tile()
+            nc.sync.dma_start(
+                out=r[:],
+                in_=mv2[512 * c : 512 * c + 512, 512 * g : 512 * g + 512].rearrange("(p j) w -> p j w", j=4),
+            )
+            mraw[g, c] = r[:]
+
+        for what in LOADS.split():
+            if what[0] == "a":
+                load_a(int(what[1]))
+            elif what == "ms":
+                nc.sync.dma_start(out=msb[:], in_=ms.rearrange("b (g p k) -> p (b g) k", g=4, k=4))
+            elif what == "mk":
+                nc.sync.dma_start(out=mksb[:], in_=mksq2)
+            elif what == "qe":
+                nc.sync.dma_start(out=qesb[:], in_=qe2)
+            else:
+                load_mv(int(what[1]), int(what[2]))
+
+        ident = keep.tile([128, 128], F32, name="ident", tag="ident", align_bytes=64)
+        make_identity(nc, ident[:])
+
+        gc = [codes("gc%d" % c) for c in range(3)]
+        ggrp = []
+        for c in range(3):
+            x = grp_tile()
+            ggrp.append(x)
+            eng = S.copy if c == 1 else V.tensor_copy
+            eng(
+                out=x[:].rearrange("p (t m j) -> p t m j", t=4, j=4),
+                in_=graw[c][:].rearrange("p j (m t) -> p t m j", t=4),
+            )
+
+        def quant_g(k):
+            V.quantize_mx(out=gc[k][0][:].bitcast(E5), scales=gc[k][1][:], in_=ggrp[k][:])
+
+        msn = keep.tile([128, 16], F32, name="msn", tag="msn")
+
+        mc = {}
+        mgrp = {}
+        dasb = {}
+        part = keep.tile([128, 16], F32, name="part", tag="part")
+        at = {}
+        dab = {}
+
+        def regroup(eng, x, src, lo, hi):
+            eng(
+                out=x[:, 4 * lo : 4 * hi].rearrange("p (c i t) -> p c t i", i=4, t=4),
+                in_=src[:, :, lo:hi].rearrange("p t (c i) -> p c t i", i=4),
+            )
+
+        def inter(g, c, eng, lo=0, hi=512):
+            if (g, c) not in mgrp:
+                mgrp[g, c] = grp_tile()
+            regroup(eng, mgrp[g, c], mraw[g, c], lo, hi)
+
+        def quant(g, c):
+            mc[g, c] = codes("mc%d%d" % (g, c))
+            V.quantize_mx(out=mc[g, c][0][:].bitcast(E4), scales=mc[g, c][1][:], in_=mgrp[g, c][:])
+
+        def trans(g, t, src):
+            b = bank("at")
+            for k in range(4):
+                T.transpose(b[:, 128 * k : 128 * k + 128], src(k, t), ident[:])
+            at[g, t] = b
+
+        def mm_da(g, c):
+            for t in range(4):
+                if c == 0:
+                    dab[g, t] = bank("da")
+                T.matmul_mx(
+                    out=dab[g, t][:],
+                    lhsT=gc[c][0][:, 128 * t : 128 * t + 128].bitcast(E5),
+                    lhsT_scale=gc[c][1][:, 128 * t : 128 * t + 128],
+                    rhs=mc[g, c][0][:].bitcast(E4),
+                    rhs_scale=mc[g, c][1][:],
+                    start=(c == 0),
+                    stop=(c == 2),
+                )
+
+        def da_copy(g, t):
+            x = keep.tile([128, 512], F32, name="dasb%d%d" % (g, t), tag="dasb%d%d" % (g, t), align_bytes=64)
+            S.copy(out=x[:], in_=dab[g, t][:])
+            dasb[g, t] = x
+
+        def v1(g, t):
+            j = rot.tile([128, 512], BF16, name="junk", tag="junk", bufs=2)
+            V.scalar_tensor_tensor(
+                out=j[:].rearrange("p (n k) -> p n k", k=4),
+                in0=dasb[g, t][:].rearrange("p (n k) -> p n k", k=4),
+                scalar=1.0,
+                in1=at[g, t][:].rearrange("p (k n) -> p n k", k=4),
+                op0=ALU.mult,
+                op1=ALU.mult,
+                accum_out=part[:, 4 * t + g : 4 * t + g + 1],
+            )
+
+        apr = {}
+
+        def aprime(g):
+            x = rot.tile([128, 4, 4, 128], F32, name="apr", tag="aff", bufs=6, align_bytes=64)
+            for k in range(4):
+                (nc.gpsimd if APE == "G" else V).tensor_scalar(
+                    out=x[:, k, :, :],
+                    in0=araw[g][:, k, :].rearrange("p (m t) -> p t m", t=4),
+                    scalar1=msn[:, 4 * g + k : 4 * g + k + 1],
+                    scalar2=1.0,
+                    op0=ALU.mult,
+                    op1=ALU.mult,
+                )
+            apr[g] = x
+
+        def a_src(g):
+            return lambda k, t: araw[g][:, k, t:512:4]
+
+        def ap_src(g):
+            return lambda k, t: apr[g][:, k, t, :]
+
+        for g in range(5):
+            h = g - 1
+            for tok in SEQ1.split():
+                k = tok[0]
+                if k in "ABCDQ" and g == 4:
+                    continue
+                if k in "tmdvP" and h < 0:
+                    continue
+                if k == "A":
+                    inter(g, 0, V.tensor_copy)
+                    if g == 0:
+                        quant_g(0)
+                        quant_g(1)
+                        quant_g(2)
+                elif k == "B":
+                    inter(g, 1, S.copy)
+                elif k == "C":
+                    inter(g, 2, V.tensor_copy, 0, C2V)
+                elif k == "D":
+                    inter(g, 2, S.copy, C2V, 512)
+                elif k == "Q":
+                    quant(g, int(tok[1]))
+                elif k == "T":
+                    if g < 4:
+                        trans(g, int(tok[1]), a_src(g))
+                elif k == "t":
+                    trans(h, int(tok[1]), a_src(h))
+                elif k == "m":
+                    mm_da(h, int(tok[1]))
+                elif k == "n":
+                    if g < 4:
+                        mm_da(g, int(tok[1]))
+                elif k == "d":
+                    da_copy(h, int(tok[1]))
+                elif k == "v":
+                    v1(h, int(tok[1]))
+                elif k == "P":
+                    V.tensor_scalar(
+                        out=msn[:, 4 * h : 4 * h + 4],
+                        in0=msb[:, h, :],
+                        scalar1=-1.0 / (CK ** 0.5),
+                        scalar2=None,
+                        op0=ALU.mult,
+                    )
+                    if h in APG:
+                        aprime(APG[h])
+
+        mkg = rot.tile([128, 2048], BF16, name="mkg", tag="grp", bufs=5, align_bytes=64)
+        qeg = keep.tile([128, 512], BF16, name="qeg", tag="qeg", align_bytes=64)
+        mkw = mksb[:].bitcast(F32)
+        qew = qesb[:].bitcast(F32)
+        for h in range(2):
+            b = bank("da")
+            for i in range(2):
+                for u in range(2):
+                    g = 2 * h + i
+                    T.transpose(
+                        b[:, 128 * (2 * i + u) : 128 * (2 * i + u) + 128], mkw[:, 256 * g + u : 256 * g + 256 : 2], ident[:]
+                    )
+            S.copy(
+                out=mkg[:].bitcast(F32)[:, 512 * h : 512 * h + 512].rearrange("p (g c u) -> p g c u", g=2, u=2),
+                in_=b[:].rearrange("p (g u c) -> p g c u", g=2, u=2),
+            )
+        b = bank("da")
+        for u in range(2):
+            T.transpose(b[:, 128 * u : 128 * u + 128], qew[:, u:256:2], ident[:])
+        S.copy(
+            out=qeg[:].bitcast(F32).rearrange("p (c u) -> p c u", u=2),
+            in_=b[:, 0:256].rearrange("p (u c) -> p c u", u=2),
+        )
+        s = keep.tile([128, 4], F32, name="s", tag="s")
+        V.tensor_reduce(out=s[:], in_=part[:].rearrange("p (t g) -> p t g", g=4), axis=AX.X, op=ALU.add)
+
+        dzt, dzi, dzn, o1b = {}, {}, {}, {}
+
+        def v2(g, t):
+            if t == 0:
+                dzt[g] = raw_tile()
+            V.scalar_tensor_tensor(
+                out=dzt[g][:, t, :].rearrange("p (n k) -> p n k", k=4),
+                in0=dasb[g, t][:].rearrange("p (n k) -> p n k", k=4),
+                scalar=s[:, t : t + 1],
+                in1=at[g, t][:].rearrange("p (k n) -> p n k", k=4),
+                op0=ALU.subtract,
+                op1=ALU.mult,
+            )
+
+        def g_copy(out, in_):
+            nc.gpsimd.tensor_scalar(out=out, in0=in_, scalar1=1.0, scalar2=1.0, op0=ALU.mult, op1=ALU.mult)
+
+        def dz_inter(g, parts):
+            if g not in dzi:
+                dzi[g] = grp_tile()
+            x = dzi[g]
+            for eng, lo, hi in parts:
+                regroup(eng, x, dzt[g], lo, hi)
+
+        wb = {}
+
+        def dz_words(g, h):
+            b = bank("da")
+            wb[g, h] = b
+            for i in range(2):
+                w = dzt[g][:, 2 * h + i, :].bitcast(F32)
+                for u in range(2):
+                    T.transpose(b[:, 128 * (2 * i + u) : 128 * (2 * i + u) + 128], w[:, u:256:2], ident[:])
+
+        def dz_wcopy(g, h, eng):
+            if h == 0:
+                dzn[g] = grp_tile()
+            eng(
+                out=dzn[g][:].bitcast(F32)[:, 512 * h : 512 * h + 512].rearrange("p (t m u) -> p t m u", t=2, u=2),
+                in_=wb[g, h][:].rearrange("p (t u m) -> p t m u", t=2, u=2),
+            )
+
+        def dz_quant(src, nm):
+            c = rot.tile([128, 512], U32, name=nm, tag=nm, bufs=2, align_bytes=64)
+            sc = rot.tile([128, 512], U8, name=nm + "s", tag=nm + "s", bufs=2, align_bytes=64)
+            V.quantize_mx(out=c[:].bitcast(E5), scales=sc[:], in_=src[:])
+            return c, sc
+
+        zn, zi = {}, {}
+        acc = []
+
+        def out1(g):
+            c, sc = zn[g]
+            T.matmul_mx(
+                out=acc[0][:],
+                lhsT=mkc[0][:, 128 * g : 128 * g + 128].bitcast(E4),
+                lhsT_scale=mkc[1][:, 128 * g : 128 * g + 128],
+                rhs=c[:].bitcast(E5),
+                rhs_scale=sc[:],
+                start=(g == 0),
+                stop=(g == 3),
+            )
+
+        ob = {}
+
+        def out0(g):
+            c, sc = zi[g]
+            b = bank("da")
+            T.matmul_mx(
+                out=b[:], lhsT=qec[:].bitcast(E4), lhsT_scale=qecs[:], rhs=c[:].bitcast(E5), rhs_scale=sc[:],
+                start=True, stop=True,
+            )
+            ob[g] = b
+
+        def out0_store(g):
+            x = rot.tile([128, 512], F32, name="ob", tag="ob", bufs=2, align_bytes=64)
+            S.copy(out=x[:], in_=ob[g][:])
+            nc.sync.dma_start(out=o0[:, 512 * g : 512 * g + 512], in_=x[:])
+
+        mkc = codes("mkc")
+        qec = keep.tile([128, 128], U32, name="qec", tag="qec", align_bytes=64)
+        qecs = keep.tile([128, 128], U8, name="qecs", tag="qecs", align_bytes=64)
+        for t in range(4):
+            trans(0, t, ap_src(0))
+        for g in range(5):
+            h = g - 1
+            for tok in SEQ2.split():
+                k = tok[0]
+                if k in "xwWIJ" and g == 4:
+                    continue
+                if k == "p" and g > 2:
+                    continue
+                if k in "NZaoO" and h < 0:
+                    continue
+                if k == "x":
+                    v2(g, int(tok[1]))
+                elif k == "A":
+                    if g in AP2:
+                        aprime(AP2[g])
+                elif k == "M":
+                    if g == 0:
+                        V.quantize_mx(out=mkc[0][:].bitcast(E4), scales=mkc[1][:], in_=mkg[:])
+                        V.quantize_mx(out=qec[:].bitcast(E4), scales=qecs[:], in_=qeg[:])
+                elif k == "w":
+                    dz_words(g, int(tok[1]))
+                elif k == "W":
+                    dz_wcopy(g, int(tok[1]), V.tensor_copy if (g, int(tok[1])) in WV else S.copy)
+                elif k == "p":
+                    trans(g + 1, int(tok[1]), ap_src(g + 1))
+                elif k == "N":
+                    zn[h] = dz_quant(dzn[h], "zn")
+                elif k == "Z":
+                    zi[h] = dz_quant(dzi[h], "zi")
+                elif k == "a":
+                    if h == 0:
+                        acc.append(psum.tile([128, 512], F32, name="acc", tag="da", bufs=4))
+                    out1(h)
+                elif k == "o":
+                    out0(h)
+                elif k == "I":
+                    n = IV.get(g, 0)
+                    if n < 512:
+                        dz_inter(g, [(S.copy, n, 512)])
+                elif k == "J":
+                    n = IV.get(g, 0)
+                    e = V.tensor_copy if g == 3 else g_copy
+                    if n:
+                        dz_inter(g, [(e, 0, n)])
+                elif k == "O":
+                    out0_store(h)
+        x = rot.tile([128, 512], F32, name="ob", tag="ob", bufs=2, align_bytes=64)
+        V.tensor_copy(out=x[:].rearrange("p (m t) -> p m t", t=4), in_=acc[0][:].rearrange("p (t m) -> p m t", t=4))
+        nc.sync.dma_start(out=o1, in_=x[:])

@@ -102,8 +102,8 @@ def tile_vidsam_pa_v_kernel(tc, mk, mksq, qk, qe, qks, ms, mv, aff, gout, out_0,
             ggrp.append(x)
             eng = S.copy if c == 1 else V.tensor_copy
             eng(
-                out=x[:].rearrange("p (t m j) -> p t m j", t=4, j=4),
-                in_=graw[c][:].rearrange("p j (m t) -> p t m j", t=4),
+                out=x[:].rearrange("p (t m j) -> p m j t", t=4, j=4),
+                in_=graw[c][:].rearrange("p j (m t) -> p m j t", t=4),
             )
 
         def quant_g(k):
@@ -155,16 +155,18 @@ def tile_vidsam_pa_v_kernel(tc, mk, mksq, qk, qe, qks, ms, mv, aff, gout, out_0,
 
         def da_copy(g, t):
             x = keep.tile([128, 512], F32, name="dasb%d%d" % (g, t), tag="dasb%d%d" % (g, t), align_bytes=64)
-            S.copy(out=x[:], in_=dab[g, t][:])
+            S.copy(
+                out=x[:].rearrange("p (k n) -> p k n", k=4), in_=dab[g, t][:].rearrange("p (n k) -> p k n", k=4)
+            )
             dasb[g, t] = x
 
         def v1(g, t):
             j = rot.tile([128, 512], BF16, name="junk", tag="junk", bufs=2)
             V.scalar_tensor_tensor(
-                out=j[:].rearrange("p (n k) -> p n k", k=4),
-                in0=dasb[g, t][:].rearrange("p (n k) -> p n k", k=4),
+                out=j[:],
+                in0=dasb[g, t][:],
                 scalar=1.0,
-                in1=at[g, t][:].rearrange("p (k n) -> p n k", k=4),
+                in1=at[g, t][:],
                 op0=ALU.mult,
                 op1=ALU.mult,
                 accum_out=part[:, 4 * t + g : 4 * t + g + 1],
@@ -176,8 +178,8 @@ def tile_vidsam_pa_v_kernel(tc, mk, mksq, qk, qe, qks, ms, mv, aff, gout, out_0,
             x = rot.tile([128, 4, 4, 128], F32, name="apr", tag="aff", bufs=6, align_bytes=64)
             for k in range(4):
                 (nc.gpsimd if APE == "G" else V).tensor_scalar(
-                    out=x[:, k, :, :],
-                    in0=araw[g][:, k, :].rearrange("p (m t) -> p t m", t=4),
+                    out=x[:, k, :, :].rearrange("p t m -> p m t"),
+                    in0=araw[g][:, k, :].rearrange("p (m t) -> p m t", t=4),
                     scalar1=msn[:, 4 * g + k : 4 * g + k + 1],
                     scalar2=1.0,
                     op0=ALU.mult,
@@ -269,14 +271,15 @@ def tile_vidsam_pa_v_kernel(tc, mk, mksq, qk, qe, qks, ms, mv, aff, gout, out_0,
         def v2(g, t):
             if t == 0:
                 dzt[g] = raw_tile()
-            V.scalar_tensor_tensor(
-                out=dzt[g][:, t, :].rearrange("p (n k) -> p n k", k=4),
-                in0=dasb[g, t][:].rearrange("p (n k) -> p n k", k=4),
-                scalar=s[:, t : t + 1],
-                in1=at[g, t][:].rearrange("p (k n) -> p n k", k=4),
-                op0=ALU.subtract,
-                op1=ALU.mult,
-            )
+            for u in range(2):
+                V.scalar_tensor_tensor(
+                    out=dzt[g][:, t, 256 * u : 256 * u + 256].rearrange("p (n e) -> p n e", e=2),
+                    in0=dasb[g, t][:].rearrange("p (u e n) -> p u n e", u=2, e=2)[:, u, :, :],
+                    scalar=s[:, t : t + 1],
+                    in1=at[g, t][:].rearrange("p (u e n) -> p u n e", u=2, e=2)[:, u, :, :],
+                    op0=ALU.subtract,
+                    op1=ALU.mult,
+                )
 
         def g_copy(out, in_):
             nc.gpsimd.tensor_scalar(out=out, in0=in_, scalar1=1.0, scalar2=1.0, op0=ALU.mult, op1=ALU.mult)
@@ -296,7 +299,7 @@ def tile_vidsam_pa_v_kernel(tc, mk, mksq, qk, qe, qks, ms, mv, aff, gout, out_0,
             for i in range(2):
                 w = dzt[g][:, 2 * h + i, :].bitcast(F32)
                 for u in range(2):
-                    T.transpose(b[:, 128 * (2 * i + u) : 128 * (2 * i + u) + 128], w[:, u:256:2], ident[:])
+                    T.transpose(b[:, 128 * (2 * i + u) : 128 * (2 * i + u) + 128], w[:, 128 * u : 128 * u + 128], ident[:])
 
         def dz_wcopy(g, h, eng):
             if h == 0:
@@ -339,8 +342,11 @@ def tile_vidsam_pa_v_kernel(tc, mk, mksq, qk, qe, qks, ms, mv, aff, gout, out_0,
             ob[g] = b
 
         def out0_store(g):
-            x = rot.tile([128, 512], F32, name="ob", tag="ob", bufs=2, align_bytes=64)
-            S.copy(out=x[:], in_=ob[g][:])
+            x = rot.tile([128, 512], F32, name="ob", tag="ob", bufs=4, align_bytes=64)
+            S.copy(
+                out=x[:].rearrange("p (n u e) -> p n u e", u=2, e=2),
+                in_=ob[g][:].rearrange("p (u n e) -> p n u e", u=2, e=2),
+            )
             nc.sync.dma_start(out=o0[:, 512 * g : 512 * g + 512], in_=x[:])
 
         mkc = codes("mkc")
@@ -394,6 +400,6 @@ def tile_vidsam_pa_v_kernel(tc, mk, mksq, qk, qe, qks, ms, mv, aff, gout, out_0,
                         dz_inter(g, [(e, 0, n)])
                 elif k == "O":
                     out0_store(h)
-        x = rot.tile([128, 512], F32, name="ob", tag="ob", bufs=2, align_bytes=64)
+        x = keep.tile([128, 512], F32, name="ob1", tag="ob1", align_bytes=64)
         V.tensor_copy(out=x[:].rearrange("p (m t) -> p m t", t=4), in_=acc[0][:].rearrange("p (t m) -> p m t", t=4))
         nc.sync.dma_start(out=o1, in_=x[:])

from contextlib import ExitStack

import concourse.mybir as mybir
from concourse.masks import make_identity

F32 = mybir.dt.float32
BF16 = mybir.dt.bfloat16
U32 = mybir.dt.uint32
U8 = mybir.dt.uint8
E4 = mybir.dt.float8_e4m3fn_x4
E5 = mybir.dt.float8_e5m2_x4
ALU = mybir.AluOpType
AX = mybir.AxisListType

C, N, P, CK = 1536, 2048, 512, 128
FLOPS = 2 * N * P * C + 2 * 2 * CK * P * N
BYTES = 2 * (CK * N + CK * P + N + C * N + C * P) + 4 * (N * P + CK * N + CK * P)
C2V = 128
RAWB = 15
LOADS = "m00 ms m01 m02 m12 m11 m10 a0 m20 m21 m22 a1 m30 m31 m32 a2 mk a3 qe"
SEQ1 = "t0 t1 B A C P Q0 d0 Q1 d1 D t2 d2 d3 t3 n0 v0 n1 v1 Q2 v2 v3 n2"
APG = {1: 0, 2: 1, 3:2}
SEQ2 = "x0 x1 M w0 x2 x3 W0 A Z N p1 J p0 p3 p2 o w1 I O a W1"
AP2 = {0: 3}
WV = {(3, 1)}
IV = {3: 512-64}
APE = "V"


def tile_vidsam_pa_v_kernel(tc, mk, mksq, qk, qe, qks, ms, mv, aff, gout, out_0, out_1):
    nc = tc.nc
    V, S, T = nc.vector, nc.scalar, nc.tensor
    mksq2 = mksq.rearrange("b c n -> (b c) n")
    qe2 = qe.rearrange("b c n -> (b c) n")
    mv2 = mv.rearrange("b c n -> (b c) n")
    g2 = gout.rearrange("b c n -> (b c) n")
    a2 = aff.rearrange("b c n -> (b c) n")
    o0 = out_0.rearrange("b c n -> (b c) n")
    o1 = out_1.rearrange("b c n -> (b c) n")
    with ExitStack() as ctx:
        keep = ctx.enter_context(tc.tile_pool(name="keep", bufs=1))
        rot = ctx.enter_context(tc.tile_pool(name="rot", bufs=2))
        psum = ctx.enter_context(tc.psum_pool(name="psum", bufs=4))
        ctx.enter_context(tc.manual_schedule())

        def bank(tag):
            return psum.tile([128, 512], F32, name=tag, tag=tag, bufs=4)

        def raw_tile():
            return rot.tile([128, 4, 512], BF16, name="raw", tag="raw", bufs=RAWB, align_bytes=64)

        def grp_tile():
            return rot.tile([128, 2048], BF16, name="grp", tag="grp", bufs=5, align_bytes=64)

        def codes(name):
            c = keep.tile([128, 512], U32, name=name, tag=name, align_bytes=64)
            s = keep.tile([128, 512], U8, name=name + "s", tag=name + "s", align_bytes=64)
            return c, s

        graw, mraw, araw = [], {}, {}
        for c in range(3):
            r = raw_tile()
            nc.sync.dma_start(out=r[:], in_=g2[512 * c : 512 * c + 512, :].rearrange("(p j) w -> p j w", j=4))
            graw.append(r)

        def load_a(g):
            t = rot.tile([128, 4, 512], F32, name="aff", tag="aff", bufs=6, align_bytes=64)
            nc.sync.dma_start(out=t[:], in_=a2[512 * g : 512 * g + 512, :].rearrange("(p k) w -> p k w", k=4))
            araw[g] = t

        msb = keep.tile([128, 4, 4], BF16, name="msb", tag="msb")
        mksb = keep.tile([128, 2048], BF16, name="mksb", tag="mksb", align_bytes=64)
        qesb = keep.tile([128, 512], BF16, name="qesb", tag="qesb", align_bytes=64)

        def load_mv(g, c):
            r = raw_tile()
            nc.sync.dma_start(
                out=r[:],
                in_=mv2[512 * c : 512 * c + 512, 512 * g : 512 * g + 512].rearrange("(p j) w -> p j w", j=4),
            )
            mraw[g, c] = r[:]

        for what in LOADS.split():
            if what[0] == "a":
                load_a(int(what[1]))
            elif what == "ms":
                nc.sync.dma_start(out=msb[:], in_=ms.rearrange("b (g p k) -> p (b g) k", g=4, k=4))
            elif what == "mk":
                nc.sync.dma_start(out=mksb[:], in_=mksq2)
            elif what == "qe":
                nc.sync.dma_start(out=qesb[:], in_=qe2)
            else:
                load_mv(int(what[1]), int(what[2]))

        ident = keep.tile([128, 128], F32, name="ident", tag="ident", align_bytes=64)
        make_identity(nc, ident[:])

        gc = [codes("gc%d" % c) for c in range(3)]
        ggrp = []
        for c in range(3):
            x = grp_tile()
            ggrp.append(x)
            eng = S.copy if c == 1 else V.tensor_copy
            eng(
                out=x[:].rearrange("p (t m j) -> p m j t", t=4, j=4),
                in_=graw[c][:].rearrange("p j (m t) -> p m j t", t=4),
            )

        def quant_g(k):
            V.quantize_mx(out=gc[k][0][:].bitcast(E5), scales=gc[k][1][:], in_=ggrp[k][:])

        msn = keep.tile([128, 16], F32, name="msn", tag="msn")

        mc = {}
        mgrp = {}
        dasb = {}
        part = keep.tile([128, 16], F32, name="part", tag="part")
        at = {}
        dab = {}

        def regroup(eng, x, src, lo, hi):
            eng(
                out=x[:, 4 * lo : 4 * hi].rearrange("p (c i t) -> p c t i", i=4, t=4),
                in_=src[:, :, lo:hi].rearrange("p t (c i) -> p c t i", i=4),
            )

        def inter(g, c, eng, lo=0, hi=512):
            if (g, c) not in mgrp:
                mgrp[g, c] = grp_tile()
            regroup(eng, mgrp[g, c], mraw[g, c], lo, hi)

        def quant(g, c):
            mc[g, c] = codes("mc%d%d" % (g, c))
            V.quantize_mx(out=mc[g, c][0][:].bitcast(E4), scales=mc[g, c][1][:], in_=mgrp[g, c][:])

        def trans(g, t, src):
            b = bank("at")
            for k in range(4):
                T.transpose(b[:, 128 * k : 128 * k + 128], src(k, t), ident[:])
            at[g, t] = b

        def mm_da(g, c):
            for t in range(4):
                if c == 0:
                    dab[g, t] = bank("da")
                T.matmul_mx(
                    out=dab[g, t][:],
                    lhsT=gc[c][0][:, 128 * t : 128 * t + 128].bitcast(E5),
                    lhsT_scale=gc[c][1][:, 128 * t : 128 * t + 128],
                    rhs=mc[g, c][0][:].bitcast(E4),
                    rhs_scale=mc[g, c][1][:],
                    start=(c == 0),
                    stop=(c == 2),
                )

        def da_copy(g, t):
            x = keep.tile([128, 512], F32, name="dasb%d%d" % (g, t), tag="dasb%d%d" % (g, t), align_bytes=64)
            S.copy(
                out=x[:].rearrange("p (k n) -> p k n", k=4), in_=dab[g, t][:].rearrange("p (n k) -> p k n", k=4)
            )
            dasb[g, t] = x

        def v1(g, t):
            j = rot.tile([128, 512], BF16, name="junk", tag="junk", bufs=2)
            V.scalar_tensor_tensor(
                out=j[:],
                in0=dasb[g, t][:],
                scalar=1.0,
                in1=at[g, t][:],
                op0=ALU.mult,
                op1=ALU.mult,
                accum_out=part[:, 4 * t + g : 4 * t + g + 1],
            )

        apr = {}

        def aprime(g):
            x = rot.tile([128, 4, 4, 128], F32, name="apr", tag="aff", bufs=6, align_bytes=64)
            for k in range(4):
                (nc.gpsimd if APE == "G" else V).tensor_scalar(
                    out=x[:, k, :, :].rearrange("p t m -> p m t"),
                    in0=araw[g][:, k, :].rearrange("p (m t) -> p m t", t=4),
                    scalar1=msn[:, 4 * g + k : 4 * g + k + 1],
                    scalar2=1.0,
                    op0=ALU.mult,
                    op1=ALU.mult,
                )
            apr[g] = x

        def a_src(g):
            return lambda k, t: araw[g][:, k, t:512:4]

        def ap_src(g):
            return lambda k, t: apr[g][:, k, t, :]

        for g in range(5):
            h = g - 1
            for tok in SEQ1.split():
                k = tok[0]
                if k in "ABCDQ" and g == 4:
                    continue
                if k in "tmdvP" and h < 0:
                    continue
                if k == "A":
                    inter(g, 0, V.tensor_copy)
                    if g == 0:
                        quant_g(0)
                        quant_g(1)
                        quant_g(2)
                elif k == "B":
                    inter(g, 1, S.copy)
                elif k == "C":
                    inter(g, 2, V.tensor_copy, 0, C2V)
                elif k == "D":
                    inter(g, 2, S.copy, C2V, 512)
                elif k == "Q":
                    quant(g, int(tok[1]))
                elif k == "T":
                    if g < 4:
                        trans(g, int(tok[1]), a_src(g))
                elif k == "t":
                    trans(h, int(tok[1]), a_src(h))
                elif k == "m":
                    mm_da(h, int(tok[1]))
                elif k == "n":
                    if g < 4:
                        mm_da(g, int(tok[1]))
                elif k == "d":
                    da_copy(h, int(tok[1]))
                elif k == "v":
                    v1(h, int(tok[1]))
                elif k == "P":
                    V.tensor_scalar(
                        out=msn[:, 4 * h : 4 * h + 4],
                        in0=msb[:, h, :],
                        scalar1=-1.0 / (CK ** 0.5),
                        scalar2=None,
                        op0=ALU.mult,
                    )
                    if h in APG:
                        aprime(APG[h])

        mkg = rot.tile([128, 2048], BF16, name="mkg", tag="grp", bufs=5, align_bytes=64)
        qeg = keep.tile([128, 512], BF16, name="qeg", tag="qeg", align_bytes=64)
        mkw = mksb[:].bitcast(F32)
        qew = qesb[:].bitcast(F32)
        for h in range(2):
            b = bank("da")
            for i in range(2):
                for u in range(2):
                    g = 2 * h + i
                    T.transpose(
                        b[:, 128 * (2 * i + u) : 128 * (2 * i + u) + 128], mkw[:, 256 * g + u : 256 * g + 256 : 2], ident[:]
                    )
            S.copy(
                out=mkg[:].bitcast(F32)[:, 512 * h : 512 * h + 512].rearrange("p (g c u) -> p g c u", g=2, u=2),
                in_=b[:].rearrange("p (g u c) -> p g c u", g=2, u=2),
            )
        b = bank("da")
        for u in range(2):
            T.transpose(b[:, 128 * u : 128 * u + 128], qew[:, u:256:2], ident[:])
        S.copy(
            out=qeg[:].bitcast(F32).rearrange("p (c u) -> p c u", u=2),
            in_=b[:, 0:256].rearrange("p (u c) -> p c u", u=2),
        )
        s = keep.tile([128, 4], F32, name="s", tag="s")
        V.tensor_reduce(out=s[:], in_=part[:].rearrange("p (t g) -> p t g", g=4), axis=AX.X, op=ALU.add)

        dzt, dzi, dzn, o1b = {}, {}, {}, {}

        def v2(g, t):
            if t == 0:
                dzt[g] = raw_tile()
            for u in range(2):
                V.scalar_tensor_tensor(
                    out=dzt[g][:, t, 256 * u : 256 * u + 256].rearrange("p (n e) -> p n e", e=2),
                    in0=dasb[g, t][:].rearrange("p (u e n) -> p u n e", u=2, e=2)[:, u, :, :],
                    scalar=s[:, t : t + 1],
                    in1=at[g, t][:].rearrange("p (u e n) -> p u n e", u=2, e=2)[:, u, :, :],
                    op0=ALU.subtract,
                    op1=ALU.mult,
                )

        def g_copy(out, in_):
            nc.gpsimd.tensor_scalar(out=out, in0=in_, scalar1=1.0, scalar2=1.0, op0=ALU.mult, op1=ALU.mult)

        def dz_inter(g, parts):
            if g not in dzi:
                dzi[g] = grp_tile()
            x = dzi[g]
            for eng, lo, hi in parts:
                regroup(eng, x, dzt[g], lo, hi)

        wb = {}

        def dz_words(g, h):
            b = bank("da")
            wb[g, h] = b
            for i in range(2):
                w = dzt[g][:, 2 * h + i, :].bitcast(F32)
                for u in range(2):
                    T.transpose(b[:, 128 * (2 * i + u) : 128 * (2 * i + u) + 128], w[:, 128 * u : 128 * u + 128], ident[:])

        def dz_wcopy(g, h, eng):
            if h == 0:
                dzn[g] = grp_tile()
            eng(
                out=dzn[g][:].bitcast(F32)[:, 512 * h : 512 * h + 512].rearrange("p (t m u) -> p t m u", t=2, u=2),
                in_=wb[g, h][:].rearrange("p (t u m) -> p t m u", t=2, u=2),
            )

        def dz_quant(src, nm):
            c = rot.tile([128, 512], U32, name=nm, tag=nm, bufs=2, align_bytes=64)
            sc = rot.tile([128, 512], U8, name=nm + "s", tag=nm + "s", bufs=2, align_bytes=64)
            V.quantize_mx(out=c[:].bitcast(E5), scales=sc[:], in_=src[:])
            return c, sc

        zn, zi = {}, {}
        acc = []

        def out1(g):
            c, sc = zn[g]
            T.matmul_mx(
                out=acc[0][:],
                lhsT=mkc[0][:, 128 * g : 128 * g + 128].bitcast(E4),
                lhsT_scale=mkc[1][:, 128 * g : 128 * g + 128],
                rhs=c[:].bitcast(E5),
                rhs_scale=sc[:],
                start=(g == 0),
                stop=(g == 3),
            )

        ob = {}

        def out0(g):
            c, sc = zi[g]
            b = bank("da")
            T.matmul_mx(
                out=b[:], lhsT=qec[:].bitcast(E4), lhsT_scale=qecs[:], rhs=c[:].bitcast(E5), rhs_scale=sc[:],
                start=True, stop=True,
            )
            ob[g] = b

        def out0_store(g):
            x = rot.tile([128, 512], F32, name="ob", tag="ob", bufs=4, align_bytes=64)
            S.copy(
                out=x[:].rearrange("p (n u e) -> p n u e", u=2, e=2),
                in_=ob[g][:].rearrange("p (u n e) -> p n u e", u=2, e=2),
            )
            nc.sync.dma_start(out=o0[:, 512 * g : 512 * g + 512], in_=x[:])

        mkc = codes("mkc")
        qec = keep.tile([128, 128], U32, name="qec", tag="qec", align_bytes=64)
        qecs = keep.tile([128, 128], U8, name="qecs", tag="qecs", align_bytes=64)
        for t in range(4):
            trans(0, t, ap_src(0))
        for g in range(5):
            h = g - 1
            for tok in SEQ2.split():
                k = tok[0]
                if k in "xwWIJ" and g == 4:
                    continue
                if k == "p" and g > 2:
                    continue
                if k in "NZaoO" and h < 0:
                    continue
                if k == "x":
                    v2(g, int(tok[1]))
                elif k == "A":
                    if g in AP2:
                        aprime(AP2[g])
                elif k == "M":
                    if g == 0:
                        V.quantize_mx(out=mkc[0][:].bitcast(E4), scales=mkc[1][:], in_=mkg[:])
                        V.quantize_mx(out=qec[:].bitcast(E4), scales=qecs[:], in_=qeg[:])
                elif k == "w":
                    dz_words(g, int(tok[1]))
                elif k == "W":
                    dz_wcopy(g, int(tok[1]), V.tensor_copy if (g, int(tok[1])) in WV else S.copy)
                elif k == "p":
                    trans(g + 1, int(tok[1]), ap_src(g + 1))
                elif k == "N":
                    zn[h] = dz_quant(dzn[h], "zn")
                elif k == "Z":
                    zi[h] = dz_quant(dzi[h], "zi")
                elif k == "a":
                    if h == 0:
                        acc.append(psum.tile([128, 512], F32, name="acc", tag="da", bufs=4))
                    out1(h)
                elif k == "o":
                    out0(h)
                elif k == "I":
                    n = IV.get(g, 0)
                    if n < 512:
                        dz_inter(g, [(S.copy, n, 512)])
                elif k == "J":
                    n = IV.get(g, 0)
                    e = V.tensor_copy if g == 3 else g_copy
                    if n:
                        dz_inter(g, [(e, 0, n)])
                elif k == "O":
                    out0_store(h)
        x = keep.tile([128, 512], F32, name="ob1", tag="ob1", align_bytes=64)
        V.tensor_copy(out=x[:].rearrange("p (m t) -> p m t", t=4), in_=acc[0][:].rearrange("p (t m) -> p m t", t=4))
        nc.sync.dma_start(out=o1, in_=x[:])
